import numpy as np
import ml_dtypes


def mxq(x, axis, fmt="e4m3"):
    dtype, down = {"e4m3": (ml_dtypes.float8_e4m3fn, 7), "e5m2": (ml_dtypes.float8_e5m2, 14)}[fmt]
    v = np.moveaxis(np.asarray(x, np.float32).astype(ml_dtypes.bfloat16).astype(np.float64), axis, -1)
    blocks = v.reshape(v.shape[:-1] + (-1, 32))
    amax = np.abs(blocks).max(-1, keepdims=True)
    byte = np.maximum(np.where(amax > 0, np.frexp(amax)[1] - 1 + 127, 0) - down, 1)
    scale = np.exp2(byte - 127.0)
    codes = (blocks / scale).astype(np.float32).astype(dtype).astype(np.float64)
    return np.moveaxis((codes * scale).reshape(v.shape), -1, axis)


WIDE = False


def mx_kscale(k):
    if not WIDE:
        return np.ones(k)
    levels = np.array([10, -10, 5, -5, 0])
    if k % 512:
        return np.exp2(np.random.permutation(np.resize(levels, k // 32))).repeat(32)
    a = np.empty((k // 512, 16))
    for p in range(k // 512):
        a[p, :8] = np.random.permutation(np.resize(levels, 8))
        for g in range(8):
            far = levels[np.abs(levels - a[p, g]) >= 10]
            a[p, g + 8] = far[np.random.randint(len(far))]
    return np.exp2(a.ravel()).repeat(32)


BF16 = ml_dtypes.bfloat16


def bf(x):
    return np.asarray(x, np.float32).astype(BF16)


def f64(x):
    return np.asarray(x).astype(np.float64)


E2M1 = np.array([0.0, 0.5, 1.0, 1.5, 2.0, 3.0, 4.0, 6.0, -0.0, -0.5, -1.0, -1.5, -2.0, -3.0, -4.0, -6.0])


def pack_weight(w, fmt):
    k, n = w.shape
    w = f64(bf(w)).reshape(k // 32, 32, n)
    amax = np.abs(w).max(1)
    if fmt == "e4m3":
        byte = np.frexp(amax)[1] - 1 + 127 - 7
    else:
        mant, ex = np.frexp(amax / 6.0)
        byte = np.where(mant > 0.5, ex, ex - 1) + 127
    byte = np.clip(np.where(amax > 0, byte, 1), 1, 254)
    scaled = (w * np.exp2(127.0 - byte)[:, None, :]).reshape(k, n).astype(np.float32)
    by_word = np.ascontiguousarray(scaled.reshape(k // 512, 128, 4, n).transpose(0, 1, 3, 2))
    if fmt == "e4m3":
        words = by_word.astype(ml_dtypes.float8_e4m3fn).view(np.uint8)
    else:
        c = by_word.astype(ml_dtypes.float4_e2m1fn).view(np.uint8) & 0xF
        words = c[..., 0::2] | (c[..., 1::2] << 4)
    return np.ascontiguousarray(words), np.ascontiguousarray(byte.astype(np.uint8).reshape(k // 512, 16, n))


def unpack_weight(words, scales, fmt):
    g, p, n, _ = words.shape
    if fmt == "e4m3":
        vals = np.ascontiguousarray(words).view(ml_dtypes.float8_e4m3fn).astype(np.float64)
    else:
        nib = np.empty((g, p, n, 4), np.uint8)
        nib[..., 0::2] = words & 0xF
        nib[..., 1::2] = words >> 4
        vals = E2M1[nib]
    vals = vals * np.repeat(np.exp2(scales.astype(np.float64) - 127.0), 8, axis=1)[..., None]
    return vals.transpose(0, 1, 3, 2).reshape(g * 512, n)
def pack4(w):
    words, scales = pack_weight(w, "e2m1")
    return words.reshape(words.shape[0], 128, -1), scales


def unpack4(words, scales):
    return unpack_weight(words.reshape(words.shape[0], 128, -1, 2), scales, "e2m1")


S, E, C, HD, HP = 2048, 768, 256, 1024, 1024
R = 2 * HP


def sigmoid(v):
    return 1.0 / (1.0 + np.exp(-v))


def draw0():
    s, t = mx_kscale(R), mx_kscale(HD)
    r = bf(np.abs(np.random.standard_normal((C, R))) * 0.5 * s)
    psi_w1_words, psi_w1_scales = pack4((np.random.standard_normal((HD, R)) * 2.0 / np.sqrt(R) / s * t[:, None]).T)
    psi_b1 = bf(np.random.standard_normal(HD) * 0.3 * t)
    w_dw_words, w_dw_scales = pack4((np.random.standard_normal((E, HD)) * 1.5 / np.sqrt(HD) / t).T)
    b_dw = bf(np.random.standard_normal(E) * 0.3)
    w_gate_words, w_gate_scales = pack4((np.random.standard_normal((E, HD)) * 1.5 / np.sqrt(HD) / t).T)
    b_gate = bf(np.random.standard_normal(E) * 0.3)
    W0 = bf(np.random.standard_normal(E) * 0.1)
    return {"r": r,
            "psi_w1_words": psi_w1_words,
            "psi_w1_scales": psi_w1_scales,
            "psi_b1": psi_b1,
            "w_dw_words": w_dw_words,
            "w_dw_scales": w_dw_scales,
            "b_dw": b_dw,
            "w_gate_words": w_gate_words,
            "w_gate_scales": w_gate_scales,
            "b_gate": b_gate,
            "W0": W0}


def core(r, psi_w1_words, psi_w1_scales, psi_b1, w_dw_words, w_dw_scales, b_dw, w_gate_words, w_gate_scales, b_gate, W0):
    hid = np.maximum((mxq(f64(r), 1, "e4m3") @ unpack4(psi_w1_words, psi_w1_scales)) + f64(psi_b1), 0.0)
    hq = mxq(hid, 1, "e4m3")
    dW = (hq @ unpack4(w_dw_words, w_dw_scales)) + f64(b_dw)
    gate = sigmoid((hq @ unpack4(w_gate_words, w_gate_scales)) + f64(b_gate))
    return f64(W0)[None, :] + gate * dW


def e4m3fn_bytes(y):
    return np.clip(np.asarray(y, np.float64), -448.0, 448.0).astype(np.float32).astype(ml_dtypes.float8_e4m3fn).view(np.uint8)


def e4m3fn_values(b):
    return np.asarray(b, np.uint8).view(ml_dtypes.float8_e4m3fn).astype(np.float64)


def setup_inputs():
    d = draw0()
    x0 = np.asarray(d['r']).astype(np.float64)
    s = (np.max(np.abs(x0), axis=(0,), keepdims=True) / 448.0).astype(np.float32)
    out = {}
    for k, v in d.items():
        if k == 'r':
            out['r_bytes'] = e4m3fn_bytes(x0 / s.astype(np.float64))
            out['r_scale'] = s
        else:
            out[k] = v
    return out


def reference(r_bytes, r_scale, psi_w1_words, psi_w1_scales, psi_b1, w_dw_words, w_dw_scales, b_dw, w_gate_words, w_gate_scales, b_gate, W0):
    return core(e4m3fn_values(r_bytes) * r_scale.astype(np.float64), psi_w1_words, psi_w1_scales, psi_b1, w_dw_words, w_dw_scales, b_dw, w_gate_words, w_gate_scales, b_gate, W0)

@@ -1,0 +1,341 @@
+from contextlib import ExitStack
+
+import concourse.mybir as mybir
+from concourse.masks import make_identity
+
+S_CLS, R, HD, E = 256, 2048, 1024, 768
+FLOPS = 2 * S_CLS * R * HD + 2 * S_CLS * HD * 2 * E
+
+F32 = mybir.dt.float32
+BF16 = mybir.dt.bfloat16
+U32 = mybir.dt.uint32
+I32 = mybir.dt.int32
+U8 = mybir.dt.uint8
+F8 = mybir.dt.float8_e4m3fn
+FP8X4 = mybir.dt.float8_e4m3fn_x4
+FP4X4 = mybir.dt.float4_e2m1fn_x4
+ACT = mybir.ActivationFunctionType
+ALU = mybir.AluOpType
+
+P = 128
+G1 = R // 512
+G2 = HD // 512
+NE = E // P
+
+
+def tile_metalinearheadml_pb_w4_kernel(
+    tc, r_bytes, r_scale, psi_w1_words, psi_w1_scales, psi_b1, w_dw_words, w_dw_scales, b_dw, w_gate_words, w_gate_scales, b_gate, W0, out
+):
+    nc = tc.nc
+    with ExitStack() as ctx:
+        keep = ctx.enter_context(tc.tile_pool(name="keep", bufs=1))
+        psum = ctx.enter_context(tc.psum_pool(name="psum", bufs=1))
+        ctx.enter_context(tc.manual_schedule())
+
+        def sb(shape, dt, name):
+            return keep.tile(shape, dt, name=name, tag=name, align_bytes=256)
+
+        def bank(i, name):
+            return psum.tile([P, 512], F32, name=name, tag="bank%d" % i)
+
+        warm = sb([P, 8], F32, "warm")
+        psi_sc = sb([P, G1, HD], U8, "psi_sc")
+        w_sc = sb([P, G2, 2 * E], U8, "w_sc")
+        rb8 = [sb([P, R], U8, "rb8_%d" % c) for c in range(2)]
+        rsc = sb([P, G1, 4], F32, "rsc")
+        psi = sb([P, G1, 2 * HD], U8, "psi")
+        b1 = sb([P, HD], BF16, "b1")
+        w = sb([P, G2, 4 * E], U8, "w")
+        bgb = sb([P, E], BF16, "bgb")
+        bdb = sb([P, E], BF16, "bdb")
+        w0b = sb([P, E], BF16, "w0b")
+        brow = sb([P, P], BF16, "brow")
+        browf = sb([P, P], F32, "browf")
+        bcol = sb([P, 3 * NE], F32, "bcol")
+        ident = sb([P, P], F32, "ident")
+
+        nc.vector.memset(warm[:], 0.0)
+        nc.scalar.activation(out=warm[:, 1:2], in_=warm[:, 0:1], func=ACT.Sigmoid)
+        nc.vector.memset(psi_sc[:].rearrange("p g n -> p (g n)").bitcast(I32), 0)
+        nc.vector.memset(w_sc[:].rearrange("p g n -> p (g n)").bitcast(I32), 0)
+        make_identity(nc, ident[:])
+        nc.gpsimd.memset(brow[:], 0.0)
+        nc.gpsimd.dma_start(out=b1[:], in_=psi_b1.partition_broadcast(P))
+        for i, vec in enumerate((b_dw, b_gate, W0)):
+            nc.gpsimd.dma_start(out=brow[NE * i : NE * (i + 1), :], in_=vec.rearrange("(j p) -> j p", p=P))
+        nc.gpsimd.tensor_copy(out=browf[:], in_=brow[:])
+
+        nc.sync.dma_start(out=rb8[0][:, 0:512], in_=r_bytes[0:P, 0:512])
+        nc.sync.dma_start(out=rb8[0][:, 512:2048], in_=r_bytes[0:P, 512:2048])
+        nc.sync.dma_start(out=rsc[:], in_=r_scale.rearrange("o (g p t) -> p (o g) t", p=P, t=4))
+        nc.sync.dma_start(out=rb8[1][:], in_=r_bytes[P : 2 * P, :])
+        for q in range(4):
+            nc.sync.dma_start(
+                out=psi_sc[32 * q : 32 * q + 4, :, :].bitcast(I32),
+                in_=psi_w1_scales[:, 4 * q : 4 * q + 4, :].rearrange("g q n -> q g n").bitcast(I32),
+            )
+        for g in range(G1):
+            nc.sync.dma_start(out=psi[:, g, :].bitcast(I32), in_=psi_w1_words[g].bitcast(I32))
+        for k, words, sc in ((0, w_gate_words, w_gate_scales), (1, w_dw_words, w_dw_scales)):
+            nc.sync.dma_start(
+                out=w[:, :, 2 * E * k : 2 * E * (k + 1)].bitcast(I32), in_=words.rearrange("g p n -> p g n").bitcast(I32)
+            )
+            for q in range(4):
+                nc.sync.dma_start(
+                    out=w_sc[32 * q : 32 * q + 4, :, E * k : E * (k + 1)].bitcast(I32),
+                    in_=sc[:, 4 * q : 4 * q + 4, :].rearrange("g q n -> q g n").bitcast(I32),
+                )
+        nc.sync.dma_start(out=bgb[:], in_=b_gate.partition_broadcast(P))
+        nc.sync.dma_start(out=bdb[:], in_=b_dw.partition_broadcast(P))
+        nc.sync.dma_start(out=w0b[:], in_=W0.partition_broadcast(P))
+
+        rbf = [sb([P, R], BF16, "rbf_%d" % c) for c in range(2)]
+        rq = sb([P, 2, G1, P], U32, "rq")
+        rqs = sb([P, 2, G1, P], U8, "rqs")
+        grp = {}
+        xt = {}
+        acc = {}
+
+        def cast(c, g, eng):
+            src = rb8[c][:, 512 * g : 512 * (g + 1)].bitcast(F8)
+            dst = rbf[c][:, 512 * g : 512 * (g + 1)]
+            if eng == "v":
+                nc.vector.tensor_copy(out=dst, in_=src)
+            else:
+                nc.scalar.copy(out=dst, in_=src)
+
+        def turn(c, g):
+            words = rbf[c][:].bitcast(F32)
+            xt[c, g] = bank(g, "xt_%d_%d" % (c, g))
+            for u in range(2):
+                nc.tensor.transpose(xt[c, g][:, P * u : P * (u + 1)], words[:, 256 * g + u : 256 * (g + 1) : 2], ident[:])
+
+        def scale(c, g):
+            grp[c, g] = sb([P, 512], BF16, "grp_%d_%d" % (c, g))
+            nc.vector.tensor_tensor(
+                out=grp[c, g][:].rearrange("p (c u e) -> p c u e", u=2, e=2),
+                in0=xt[c, g][:, 0:256].bitcast(BF16).rearrange("p (u c e) -> p c u e", u=2, e=2),
+                in1=rsc[:, g, :].rearrange("p (u e) -> p u e", e=2).unsqueeze(1).to_broadcast([P, P, 2, 2]),
+                op=ALU.mult,
+            )
+
+        def scale_s(c, g):
+            grp[c, g] = sb([P, 512], BF16, "grp_%d_%d" % (c, g))
+            dst = grp[c, g][:].rearrange("p (c t) -> p c t", t=4)
+            src = xt[c, g][:, 0:256].bitcast(BF16).rearrange("p (u c e) -> p c u e", u=2, e=2)
+            for t in range(4):
+                nc.scalar.activation(
+                    out=dst[:, :, t : t + 1], in_=src[:, :, t // 2, t % 2 : t % 2 + 1], func=ACT.Copy, scale=rsc[:, g, t : t + 1]
+                )
+
+        def quant(c, g):
+            nc.vector.quantize_mx(out=rq[:, c, g, :].bitcast(FP8X4), scales=rqs[:, c, g, :], in_=grp[c, g][:])
+
+        def stage1(c, g):
+            for h in range(2):
+                if g == 0:
+                    acc[c, h] = bank(4 + 2 * c + h, "acc_%d_%d" % (c, h))
+                nc.tensor.matmul_mx(
+                    out=acc[c, h][:],
+                    lhsT=rq[:, c, g, :].bitcast(FP8X4),
+                    lhsT_scale=rqs[:, c, g, :],
+                    rhs=psi[:, g, 1024 * h : 1024 * (h + 1)].bitcast(FP4X4),
+                    rhs_scale=psi_sc[:, g, 512 * h : 512 * (h + 1)],
+                    start=(g == 0),
+                    stop=(g == G1 - 1),
+                )
+
+        hbf = [sb([P, HD], BF16, "hbf_%d" % c) for c in range(2)]
+        hq = sb([P, G2, S_CLS], U32, "hq")
+        hqs = sb([P, G2, S_CLS], U8, "hqs")
+        ht = {}
+        hgrp = {}
+
+        def bias(c, h):
+            cols = slice(512 * h, 512 * (h + 1))
+            nc.vector.tensor_tensor(out=hbf[c][:, cols], in0=acc[c, h][:], in1=b1[:, cols], op=ALU.add)
+
+        def hturn(c, g, b):
+            words = hbf[c][:].bitcast(F32)
+            ht[c, g] = bank(b, "ht_%d_%d" % (c, g))
+            for u in range(2):
+                nc.tensor.transpose(ht[c, g][:, P * u : P * (u + 1)], words[:, 256 * g + u : 256 * (g + 1) : 2], ident[:])
+
+        def relu(c, g):
+            hgrp[c, g] = sb([P, 512], BF16, "hgrp_%d_%d" % (c, g))
+            nc.scalar.activation(
+                out=hgrp[c, g][:].rearrange("p (c u e) -> p c u e", u=2, e=2),
+                in_=ht[c, g][:, 0:256].bitcast(BF16).rearrange("p (u c e) -> p c u e", u=2, e=2),
+                func=ACT.Relu,
+            )
+
+        def hquant(c, g):
+            cols = slice(P * c, P * (c + 1))
+            nc.vector.quantize_mx(out=hq[:, g, cols].bitcast(FP8X4), scales=hqs[:, g, cols], in_=hgrp[c, g][:])
+
+        tg = sb([P, E], F32, "tg")
+        td = sb([P, E], F32, "td")
+
+        def wide(ps, n, g):
+            nc.tensor.matmul_mx(
+                out=ps[:],
+                lhsT=hq[:, g, 0:P].bitcast(FP8X4),
+                lhsT_scale=hqs[:, g, 0:P],
+                rhs=w[:, g, 1024 * n : 1024 * (n + 1)].bitcast(FP4X4),
+                rhs_scale=w_sc[:, g, 512 * n : 512 * (n + 1)],
+                start=(g == 0),
+                stop=(g == G2 - 1),
+            )
+
+        def addb(dst, vec, lo, hi, ps, at):
+            nc.vector.tensor_tensor(out=dst[:, lo:hi], in0=ps[:, at : at + hi - lo], in1=vec[:, lo:hi], op=ALU.add)
+
+        def finish(lo, hi):
+            nc.vector.tensor_tensor(out=td[:, lo:hi], in0=td[:, lo:hi], in1=tg[:, lo:hi], op=ALU.mult)
+            nc.gpsimd.tensor_tensor(out=osb[0][:, lo:hi], in0=td[:, lo:hi], in1=w0b[:, lo:hi], op=ALU.add)
+
+        def product(ps, slot, c, kind, j):
+            for g in range(G2):
+                col = E * kind + P * j
+                nc.tensor.matmul_mx(
+                    out=ps[:, P * slot : P * (slot + 1)],
+                    lhsT=w[:, g, 2 * col : 2 * (col + P)].bitcast(FP4X4),
+                    lhsT_scale=w_sc[:, g, col : col + P],
+                    rhs=hq[:, g, P * c : P * (c + 1)].bitcast(FP8X4),
+                    rhs_scale=hqs[:, g, P * c : P * (c + 1)],
+                    start=(g == 0),
+                    stop=(g == G2 - 1),
+                )
+
+        gate = {}
+        z = {}
+        osb = [sb([P, E], F32, "osb_%d" % c) for c in range(2)]
+
+        def sig(ps, slot, c, j):
+            gate[c, j] = sb([P, P], F32, "gate_%d_%d" % (c, j))
+            nc.scalar.activation(
+                out=gate[c, j][:], in_=ps[:, P * slot : P * (slot + 1)], func=ACT.Sigmoid, bias=bcol[:, NE + j : NE + j + 1]
+            )
+
+        def mul(ps, slot, c, j):
+            z[c, j] = sb([P, P], F32, "z_%d_%d" % (c, j))
+            nc.vector.scalar_tensor_tensor(
+                out=z[c, j][:],
+                in0=ps[:, P * slot : P * (slot + 1)],
+                scalar=bcol[:, j : j + 1],
+                in1=gate[c, j][:],
+                op0=ALU.add,
+                op1=ALU.mult,
+            )
+
+        def addw0(c, j):
+            nc.gpsimd.tensor_scalar(
+                out=z[c, j][:], in0=z[c, j][:], scalar1=1.0, scalar2=bcol[:, 2 * NE + j : 2 * NE + j + 1], op0=ALU.mult, op1=ALU.add
+            )
+
+        def back(ps, slot, c, j):
+            nc.tensor.transpose(ps[:, P * slot : P * (slot + 1)], z[c, j][:], ident[:])
+
+        cast(0, 0, "v")
+        cast(0, 1, "v")
+        cast(0, 2, "s")
+        cast(0, 3, "s")
+        for g in range(4):
+            turn(0, g)
+        for g in range(4):
+            cast(1, g, "s")
+        scale(0, 0)
+        scale(0, 1)
+        quant(0, 0)
+        turn(1, 0)
+        scale(0, 2)
+        quant(0, 1)
+        turn(1, 1)
+        stage1(0, 0)
+        stage1(0, 1)
+        scale(0, 3)
+        quant(0, 2)
+        turn(1, 2)
+        turn(1, 3)
+        scale(1, 0)
+        quant(0, 3)
+        stage1(0, 2)
+        stage1(0, 3)
+        scale(1, 1)
+        quant(1, 0)
+        bt = bank(1, "bt")
+        nc.tensor.transpose(bt[:, 0:P], browf[:], ident[:])
+        nc.scalar.copy(out=bcol[:], in_=bt[:, 0 : 3 * NE])
+        bias(0, 0)
+        quant(1, 1)
+        hturn(0, 0, 0)
+        relu(0, 0)
+        scale(1, 2)
+        stage1(1, 0)
+        bias(0, 1)
+        quant(1, 2)
+        stage1(1, 1)
+        hturn(0, 1, 1)
+        relu(0, 1)
+        scale(1, 3)
+        stage1(1, 2)
+        hquant(0, 0)
+        quant(1, 3)
+        hquant(0, 1)
+        stage1(1, 3)
+        ga = bank(4, "ga")
+        wide(ga, 0, 0)
+        wide(ga, 0, 1)
+        bias(1, 0)
+        hturn(1, 0, 2)
+        relu(1, 0)
+        gb = bank(0, "gb")
+        wide(gb, 1, 0)
+        wide(gb, 1, 1)
+        bias(1, 1)
+        hturn(1, 1, 3)
+        relu(1, 1)
+        gc = bank(5, "gc")
+        wide(gc, 2, 0)
+        wide(gc, 2, 1)
+        addb(tg, bgb, 0, 512, ga, 0)
+        hquant(1, 0)
+        addb(tg, bgb, 512, 768, gb, 0)
+        hquant(1, 1)
+        nc.scalar.activation(out=tg[:, 0:512], in_=tg[:, 0:512], func=ACT.Sigmoid)
+        nc.scalar.activation(out=tg[:, 512:768], in_=tg[:, 512:768], func=ACT.Sigmoid)
+        addb(td, bdb, 0, 256, gb, 256)
+        addb(td, bdb, 256, 768, gc, 0)
+        finish(0, 256)
+        finish(256, 512)
+        g03_1 = bank(6, "g03_1")
+        for j in range(4):
+            product(g03_1, j, 1, 0, j)
+        for j in range(4):
+            sig(g03_1, j, 1, j)
+        d03_1 = bank(7, "d03_1")
+        for j in range(4):
+            product(d03_1, j, 1, 1, j)
+        for j in range(4):
+            mul(d03_1, j, 1, j)
+        finish(512, 768)
+        nc.sync.dma_start(out=out[0:P, :], in_=osb[0][:])
+        e45_1 = bank(1, "e45_1")
+        for j in range(2):
+            product(e45_1, j, 1, 0, 4 + j)
+        for j in range(2):
+            product(e45_1, 2 + j, 1, 1, 4 + j)
+        for j in range(2):
+            sig(e45_1, j, 1, 4 + j)
+        for j in range(2):
+            mul(e45_1, 2 + j, 1, 4 + j)
+        o03_1 = bank(0, "o03_1")
+        for j in range(4):
+            back(o03_1, j, 1, j)
+        nc.vector.tensor_tensor(out=osb[1][:, 0:512], in0=o03_1[:], in1=w0b[:, 0:512], op=ALU.add)
+        nc.sync.dma_start(out=out[P : 2 * P, 0:512], in_=osb[1][:, 0:512])
+        o45_1 = bank(3, "o45_1")
+        for j in range(2):
+            back(o45_1, j, 1, 4 + j)
+        nc.vector.tensor_tensor(out=osb[1][:, 512:768], in0=o45_1[:, 0:256], in1=w0b[:, 512:768], op=ALU.add)
+        nc.sync.dma_start(out=out[P : 2 * P, 512:768], in_=osb[1][:, 512:768])

@@ -46,24 +46,25 @@ def tile_metalinearheadml_pb_w4_kernel(
         psi = sb([P, G1, 2 * HD], U8, "psi")
         b1 = sb([P, HD], BF16, "b1")
         w = sb([P, G2, 4 * E], U8, "w")
-        bgb = sb([P, E], BF16, "bgb")
-        bdb = sb([P, E], BF16, "bdb")
+        vrow = sb([P, HD], BF16, "vrow")
+        identb = sb([P, P], BF16, "identb")
         w0b = sb([P, E], BF16, "w0b")
-        brow = sb([P, P], BF16, "brow")
-        browf = sb([P, P], F32, "browf")
-        bcol = sb([P, 3 * NE], F32, "bcol")
+        zero = sb([P, 512], BF16, "zero")
+        bcol = sb([P, 3, NE], F32, "bcol")
+        one = sb([P, 1], F32, "one")
         ident = sb([P, P], F32, "ident")
 
         nc.vector.memset(warm[:], 0.0)
         nc.scalar.activation(out=warm[:, 1:2], in_=warm[:, 0:1], func=ACT.Sigmoid)
+        nc.vector.memset(zero[:], 0.0)
+        nc.vector.memset(one[:], 1.0)
+        nc.vector.memset(vrow[:], 0.0)
         nc.vector.memset(psi_sc[:].rearrange("p g n -> p (g n)").bitcast(I32), 0)
         nc.vector.memset(w_sc[:].rearrange("p g n -> p (g n)").bitcast(I32), 0)
         make_identity(nc, ident[:])
-        nc.gpsimd.memset(brow[:], 0.0)
-        nc.gpsimd.dma_start(out=b1[:], in_=psi_b1.partition_broadcast(P))
-        for i, vec in enumerate((b_dw, b_gate, W0)):
-            nc.gpsimd.dma_start(out=brow[NE * i : NE * (i + 1), :], in_=vec.rearrange("(j p) -> j p", p=P))
-        nc.gpsimd.tensor_copy(out=browf[:], in_=brow[:])
+        nc.gpsimd.dma_start(out=vrow[0:1, :], in_=psi_b1.unsqueeze(0))
+        for i, vec in enumerate((b_gate, b_dw, W0)):
+            nc.gpsimd.dma_start(out=vrow[1 + NE * i : 1 + NE * (i + 1), 0:P], in_=vec.rearrange("(j p) -> j p", p=P))
 
         nc.sync.dma_start(out=rb8[0][:, 0:512], in_=r_bytes[0:P, 0:512])
         nc.sync.dma_start(out=rb8[0][:, 512:2048], in_=r_bytes[0:P, 512:2048])
@@ -85,9 +86,17 @@ def tile_metalinearheadml_pb_w4_kernel(
                     out=w_sc[32 * q : 32 * q + 4, :, E * k : E * (k + 1)].bitcast(I32),
                     in_=sc[:, 4 * q : 4 * q + 4, :].rearrange("g q n -> q g n").bitcast(I32),
                 )
-        nc.sync.dma_start(out=bgb[:], in_=b_gate.partition_broadcast(P))
-        nc.sync.dma_start(out=bdb[:], in_=b_dw.partition_broadcast(P))
         nc.sync.dma_start(out=w0b[:], in_=W0.partition_broadcast(P))
+        nc.vector.tensor_copy(out=identb[:], in_=ident[:])
+
+        def spread(row, lo, hi, ps):
+            nc.tensor.matmul(
+                out=ps[:, 0 : hi - lo],
+                lhsT=identb[:, row : row + 1].to_broadcast([P, P]),
+                rhs=vrow[:, lo:hi],
+                start=True,
+                stop=True,
+            )
 
         rbf = [sb([P, R], BF16, "rbf_%d" % c) for c in range(2)]
         rq = sb([P, 2, G1, P], U32, "rq")
@@ -96,11 +105,20 @@ def tile_metalinearheadml_pb_w4_kernel(
         xt = {}
         acc = {}
 
+        split = set()
+
         def cast(c, g, eng):
             src = rb8[c][:, 512 * g : 512 * (g + 1)].bitcast(F8)
             dst = rbf[c][:, 512 * g : 512 * (g + 1)]
             if eng == "v":
-                nc.vector.tensor_copy(out=dst, in_=src)
+                nc.vector.tensor_scalar(
+                    out=dst.rearrange("p (u w e) -> p w u e", u=2, e=2),
+                    in0=src.rearrange("p (w u e) -> p w u e", u=2, e=2),
+                    scalar1=one[:],
+                    scalar2=None,
+                    op0=ALU.mult,
+                )
+                split.add((c, g))
             else:
                 nc.scalar.copy(out=dst, in_=src)
 
@@ -108,28 +126,32 @@ def tile_metalinearheadml_pb_w4_kernel(
             words = rbf[c][:].bitcast(F32)
             xt[c, g] = bank(g, "xt_%d_%d" % (c, g))
             for u in range(2):
-                nc.tensor.transpose(xt[c, g][:, P * u : P * (u + 1)], words[:, 256 * g + u : 256 * (g + 1) : 2], ident[:])
+                if (c, g) in split:
+                    cols = words[:, 256 * g + P * u : 256 * g + P * (u + 1)]
+                else:
+                    cols = words[:, 256 * g + u : 256 * (g + 1) : 2]
+                nc.tensor.transpose(xt[c, g][:, P * u : P * (u + 1)], cols, ident[:])
 
         def scale(c, g):
-            grp[c, g] = sb([P, 512], BF16, "grp_%d_%d" % (c, g))
+            if (c, g // 2) not in grp:
+                grp[c, g // 2] = sb([P, 2, 512], BF16, "grp_%d_%d" % (c, g // 2))
             nc.vector.tensor_tensor(
-                out=grp[c, g][:].rearrange("p (c u e) -> p c u e", u=2, e=2),
+                out=grp[c, g // 2][:, g % 2, :].rearrange("p (c u e) -> p c u e", u=2, e=2),
                 in0=xt[c, g][:, 0:256].bitcast(BF16).rearrange("p (u c e) -> p c u e", u=2, e=2),
                 in1=rsc[:, g, :].rearrange("p (u e) -> p u e", e=2).unsqueeze(1).to_broadcast([P, P, 2, 2]),
                 op=ALU.mult,
             )
 
-        def scale_s(c, g):
-            grp[c, g] = sb([P, 512], BF16, "grp_%d_%d" % (c, g))
-            dst = grp[c, g][:].rearrange("p (c t) -> p c t", t=4)
-            src = xt[c, g][:, 0:256].bitcast(BF16).rearrange("p (u c e) -> p c u e", u=2, e=2)
-            for t in range(4):
-                nc.scalar.activation(
-                    out=dst[:, :, t : t + 1], in_=src[:, :, t // 2, t % 2 : t % 2 + 1], func=ACT.Copy, scale=rsc[:, g, t : t + 1]
-                )
-
         def quant(c, g):
-            nc.vector.quantize_mx(out=rq[:, c, g, :].bitcast(FP8X4), scales=rqs[:, c, g, :], in_=grp[c, g][:])
+            nc.vector.quantize_mx(out=rq[:, c, g, :].bitcast(FP8X4), scales=rqs[:, c, g, :], in_=grp[c, g // 2][:, g % 2, :])
+
+        def quant2(c, h):
+            gs = slice(2 * h, 2 * h + 2)
+            nc.vector.quantize_mx(
+                out=rq[:, c, gs, :].rearrange("p g n -> p (g n)").bitcast(FP8X4),
+                scales=rqs[:, c, gs, :].rearrange("p g n -> p (g n)"),
+                in_=grp[c, h][:].rearrange("p g n -> p (g n)"),
+            )
 
         def stage1(c, g):
             for h in range(2):
@@ -146,20 +168,25 @@ def tile_metalinearheadml_pb_w4_kernel(
                 )
 
         hbf = [sb([P, HD], BF16, "hbf_%d" % c) for c in range(2)]
-        hq = sb([P, G2, S_CLS], U32, "hq")
-        hqs = sb([P, G2, S_CLS], U8, "hqs")
+        hq = sb([P, 2, G2, P], U32, "hq")
+        hqs = sb([P, 2, G2, P], U8, "hqs")
         ht = {}
         hgrp = {}
 
         def bias(c, h):
             cols = slice(512 * h, 512 * (h + 1))
-            nc.vector.tensor_tensor(out=hbf[c][:, cols], in0=acc[c, h][:], in1=b1[:, cols], op=ALU.add)
+            nc.vector.tensor_tensor(
+                out=hbf[c][:, cols].rearrange("p (u w e) -> p w u e", u=2, e=2),
+                in0=acc[c, h][:].rearrange("p (w u e) -> p w u e", u=2, e=2),
+                in1=b1[:, cols].rearrange("p (w u e) -> p w u e", u=2, e=2),
+                op=ALU.add,
+            )
 
         def hturn(c, g, b):
             words = hbf[c][:].bitcast(F32)
             ht[c, g] = bank(b, "ht_%d_%d" % (c, g))
             for u in range(2):
-                nc.tensor.transpose(ht[c, g][:, P * u : P * (u + 1)], words[:, 256 * g + u : 256 * (g + 1) : 2], ident[:])
+                nc.tensor.transpose(ht[c, g][:, P * u : P * (u + 1)], words[:, 256 * g + P * u : 256 * g + P * (u + 1)], ident[:])
 
         def relu(c, g):
             hgrp[c, g] = sb([P, 512], BF16, "hgrp_%d_%d" % (c, g))
@@ -170,29 +197,7 @@ def tile_metalinearheadml_pb_w4_kernel(
             )
 
         def hquant(c, g):
-            cols = slice(P * c, P * (c + 1))
-            nc.vector.quantize_mx(out=hq[:, g, cols].bitcast(FP8X4), scales=hqs[:, g, cols], in_=hgrp[c, g][:])
-
-        tg = sb([P, E], F32, "tg")
-        td = sb([P, E], F32, "td")
-
-        def wide(ps, n, g):
-            nc.tensor.matmul_mx(
-                out=ps[:],
-                lhsT=hq[:, g, 0:P].bitcast(FP8X4),
-                lhsT_scale=hqs[:, g, 0:P],
-                rhs=w[:, g, 1024 * n : 1024 * (n + 1)].bitcast(FP4X4),
-                rhs_scale=w_sc[:, g, 512 * n : 512 * (n + 1)],
-                start=(g == 0),
-                stop=(g == G2 - 1),
-            )
-
-        def addb(dst, vec, lo, hi, ps, at):
-            nc.vector.tensor_tensor(out=dst[:, lo:hi], in0=ps[:, at : at + hi - lo], in1=vec[:, lo:hi], op=ALU.add)
-
-        def finish(lo, hi):
-            nc.vector.tensor_tensor(out=td[:, lo:hi], in0=td[:, lo:hi], in1=tg[:, lo:hi], op=ALU.mult)
-            nc.gpsimd.tensor_tensor(out=osb[0][:, lo:hi], in0=td[:, lo:hi], in1=w0b[:, lo:hi], op=ALU.add)
+            nc.vector.quantize_mx(out=hq[:, c, g, :].bitcast(FP8X4), scales=hqs[:, c, g, :], in_=hgrp[c, g][:])
 
         def product(ps, slot, c, kind, j):
             for g in range(G2):
@@ -201,8 +206,8 @@ def tile_metalinearheadml_pb_w4_kernel(
                     out=ps[:, P * slot : P * (slot + 1)],
                     lhsT=w[:, g, 2 * col : 2 * (col + P)].bitcast(FP4X4),
                     lhsT_scale=w_sc[:, g, col : col + P],
-                    rhs=hq[:, g, P * c : P * (c + 1)].bitcast(FP8X4),
-                    rhs_scale=hqs[:, g, P * c : P * (c + 1)],
+                    rhs=hq[:, c, g, :].bitcast(FP8X4),
+                    rhs_scale=hqs[:, c, g, :],
                     start=(g == 0),
                     stop=(g == G2 - 1),
                 )
@@ -214,7 +219,7 @@ def tile_metalinearheadml_pb_w4_kernel(
         def sig(ps, slot, c, j):
             gate[c, j] = sb([P, P], F32, "gate_%d_%d" % (c, j))
             nc.scalar.activation(
-                out=gate[c, j][:], in_=ps[:, P * slot : P * (slot + 1)], func=ACT.Sigmoid, bias=bcol[:, NE + j : NE + j + 1]
+                out=gate[c, j][:], in_=ps[:, P * slot : P * (slot + 1)], func=ACT.Sigmoid, bias=bcol[:, 0, j : j + 1]
             )
 
         def mul(ps, slot, c, j):
@@ -222,7 +227,7 @@ def tile_metalinearheadml_pb_w4_kernel(
             nc.vector.scalar_tensor_tensor(
                 out=z[c, j][:],
                 in0=ps[:, P * slot : P * (slot + 1)],
-                scalar=bcol[:, j : j + 1],
+                scalar=bcol[:, 1, j : j + 1],
                 in1=gate[c, j][:],
                 op0=ALU.add,
                 op1=ALU.mult,
@@ -230,112 +235,162 @@ def tile_metalinearheadml_pb_w4_kernel(
 
         def addw0(c, j):
             nc.gpsimd.tensor_scalar(
-                out=z[c, j][:], in0=z[c, j][:], scalar1=1.0, scalar2=bcol[:, 2 * NE + j : 2 * NE + j + 1], op0=ALU.mult, op1=ALU.add
+                out=z[c, j][:], in0=z[c, j][:], scalar1=1.0, scalar2=bcol[:, 2, j : j + 1], op0=ALU.mult, op1=ALU.add
             )
 
         def back(ps, slot, c, j):
             nc.tensor.transpose(ps[:, P * slot : P * (slot + 1)], z[c, j][:], ident[:])
 
+        wm = bank(7, "wm")
+        nc.tensor.matmul(out=wm[:], lhsT=zero[:, 0:P], rhs=zero[:], start=True, stop=True)
+        nc.tensor.matmul(out=wm[:], lhsT=zero[:, 0:P], rhs=zero[:], start=True, stop=True)
+        nc.tensor.matmul(out=wm[:], lhsT=zero[:, 0:P], rhs=zero[:], start=True, stop=True)
         cast(0, 0, "v")
         cast(0, 1, "v")
-        cast(0, 2, "s")
         cast(0, 3, "s")
-        for g in range(4):
-            turn(0, g)
-        for g in range(4):
-            cast(1, g, "s")
+        turn(0, 0)
         scale(0, 0)
+        turn(0, 1)
+        cast(1, 1, "s")
+        nc.tensor.matmul(out=wm[:], lhsT=zero[:, 0:P], rhs=zero[:], start=True, stop=True)
+        sp1 = bank(7, "sp1")
+        spread(0, 512, 1024, sp1)
         scale(0, 1)
+        cast(0, 2, "s")
+        turn(0, 3)
         quant(0, 0)
-        turn(1, 0)
-        scale(0, 2)
-        quant(0, 1)
         turn(1, 1)
-        stage1(0, 0)
-        stage1(0, 1)
+        cast(1, 0, "s")
+        quant(0, 1)
+        turn(0, 2)
         scale(0, 3)
-        quant(0, 2)
-        turn(1, 2)
-        turn(1, 3)
-        scale(1, 0)
-        quant(0, 3)
-        stage1(0, 2)
-        stage1(0, 3)
+        nc.scalar.copy(out=b1[:, 512:1024], in_=sp1[:])
+        stage1(0, 0)
+        scale(0, 2)
+        sp0 = bank(6, "sp0")
+        spread(0, 0, 512, sp0)
+        cast(1, 2, "s")
         scale(1, 1)
+        bt = psum.tile([P, 1024], BF16, name="bt", tag="bank7")
+        nc.tensor.transpose(bt[:, 0:P], vrow[:, 0:P], identb[:])
+        turn(1, 0)
+        cast(1, 3, "s")
+        turn(1, 2)
+        quant(0, 2)
+        stage1(0, 1)
+        scale(1, 0)
+        nc.scalar.copy(out=b1[:, 0:512], in_=sp0[:])
+        stage1(0, 2)
+        quant(0, 3)
+        nc.scalar.copy(out=bcol[:], in_=bt[:, 1 : 1 + 3 * NE].rearrange("p (v j) -> p v j", v=3))
         quant(1, 0)
-        bt = bank(1, "bt")
-        nc.tensor.transpose(bt[:, 0:P], browf[:], ident[:])
-        nc.scalar.copy(out=bcol[:], in_=bt[:, 0 : 3 * NE])
-        bias(0, 0)
         quant(1, 1)
-        hturn(0, 0, 0)
-        relu(0, 0)
+        stage1(0, 3)
         scale(1, 2)
         stage1(1, 0)
         bias(0, 1)
-        quant(1, 2)
-        stage1(1, 1)
+        turn(1, 3)
+        bias(0, 0)
         hturn(0, 1, 1)
+        stage1(1, 1)
         relu(0, 1)
+        quant(1, 2)
         scale(1, 3)
+        hturn(0, 0, 0)
         stage1(1, 2)
-        hquant(0, 0)
+        relu(0, 0)
         quant(1, 3)
         hquant(0, 1)
         stage1(1, 3)
-        ga = bank(4, "ga")
-        wide(ga, 0, 0)
-        wide(ga, 0, 1)
+        hquant(0, 0)
         bias(1, 0)
-        hturn(1, 0, 2)
-        relu(1, 0)
-        gb = bank(0, "gb")
-        wide(gb, 1, 0)
-        wide(gb, 1, 1)
+        g03_0 = bank(4, "g03_0")
+        product(g03_0, 0, 0, 0, 0)
+        product(g03_0, 1, 0, 0, 1)
+        product(g03_0, 2, 0, 0, 2)
+        e45_0 = bank(0, "e45_0")
+        product(e45_0, 0, 0, 0, 4)
         bias(1, 1)
+        hturn(1, 0, 2)
+        d03_0 = bank(5, "d03_0")
+        product(d03_0, 0, 0, 1, 0)
+        relu(1, 0)
         hturn(1, 1, 3)
+        product(g03_0, 3, 0, 0, 3)
         relu(1, 1)
-        gc = bank(5, "gc")
-        wide(gc, 2, 0)
-        wide(gc, 2, 1)
-        addb(tg, bgb, 0, 512, ga, 0)
+        product(e45_0, 1, 0, 0, 5)
         hquant(1, 0)
-        addb(tg, bgb, 512, 768, gb, 0)
+        product(d03_0, 1, 0, 1, 1)
+        product(e45_0, 2, 0, 1, 4)
+        product(d03_0, 2, 0, 1, 2)
+        sig(g03_0, 1, 0, 1)
         hquant(1, 1)
-        nc.scalar.activation(out=tg[:, 0:512], in_=tg[:, 0:512], func=ACT.Sigmoid)
-        nc.scalar.activation(out=tg[:, 512:768], in_=tg[:, 512:768], func=ACT.Sigmoid)
-        addb(td, bdb, 0, 256, gb, 256)
-        addb(td, bdb, 256, 768, gc, 0)
-        finish(0, 256)
-        finish(256, 512)
+        product(d03_0, 3, 0, 1, 3)
+        sig(g03_0, 2, 0, 2)
+        product(e45_0, 3, 0, 1, 5)
+        sig(g03_0, 0, 0, 0)
         g03_1 = bank(6, "g03_1")
-        for j in range(4):
-            product(g03_1, j, 1, 0, j)
-        for j in range(4):
-            sig(g03_1, j, 1, j)
+        product(g03_1, 0, 1, 0, 0)
+        mul(d03_0, 1, 0, 1)
+        sig(g03_0, 3, 0, 3)
+        product(g03_1, 1, 1, 0, 1)
+        mul(d03_0, 0, 0, 0)
+        sig(e45_0, 0, 0, 4)
+        product(g03_1, 2, 1, 0, 2)
+        mul(d03_0, 2, 0, 2)
+        sig(e45_0, 1, 0, 5)
+        product(g03_1, 3, 1, 0, 3)
+        addw0(0, 0)
+        mul(d03_0, 3, 0, 3)
+        e45_1 = bank(2, "e45_1")
+        product(e45_1, 0, 1, 0, 4)
+        addw0(0, 2)
+        mul(e45_0, 3, 0, 5)
         d03_1 = bank(7, "d03_1")
-        for j in range(4):
-            product(d03_1, j, 1, 1, j)
-        for j in range(4):
-            mul(d03_1, j, 1, j)
-        finish(512, 768)
-        nc.sync.dma_start(out=out[0:P, :], in_=osb[0][:])
-        e45_1 = bank(1, "e45_1")
-        for j in range(2):
-            product(e45_1, j, 1, 0, 4 + j)
-        for j in range(2):
-            product(e45_1, 2 + j, 1, 1, 4 + j)
-        for j in range(2):
-            sig(e45_1, j, 1, 4 + j)
-        for j in range(2):
-            mul(e45_1, 2 + j, 1, 4 + j)
+        product(d03_1, 0, 1, 1, 0)
+        sig(g03_1, 2, 1, 2)
+        product(e45_1, 1, 1, 0, 5)
+        mul(e45_0, 2, 0, 4)
+        addw0(0, 3)
+        sig(g03_1, 3, 1, 3)
+        product(d03_1, 1, 1, 1, 1)
+        sig(g03_1, 0, 1, 0)
+        addw0(0, 4)
+        product(e45_1, 2, 1, 1, 4)
+        product(e45_1, 3, 1, 1, 5)
+        addw0(0, 5)
+        product(d03_1, 2, 1, 1, 2)
+        addw0(0, 1)
+        product(d03_1, 3, 1, 1, 3)
+        sig(e45_1, 1, 1, 5)
+        sig(e45_1, 0, 1, 4)
+        o45_0 = bank(4, "o45_0")
+        back(o45_0, 0, 0, 4)
+        back(o45_0, 1, 0, 5)
+        mul(d03_1, 2, 1, 2)
+        sig(g03_1, 1, 1, 1)
+        o03_0 = bank(1, "o03_0")
+        back(o03_0, 0, 0, 0)
+        back(o03_0, 1, 0, 1)
+        mul(d03_1, 0, 1, 0)
+        back(o03_0, 2, 0, 2)
+        nc.scalar.copy(out=osb[0][:, 512:768], in_=o45_0[:, 0:256])
+        back(o03_0, 3, 0, 3)
+        mul(d03_1, 1, 1, 1)
         o03_1 = bank(0, "o03_1")
-        for j in range(4):
-            back(o03_1, j, 1, j)
-        nc.vector.tensor_tensor(out=osb[1][:, 0:512], in0=o03_1[:], in1=w0b[:, 0:512], op=ALU.add)
-        nc.sync.dma_start(out=out[P : 2 * P, 0:512], in_=osb[1][:, 0:512])
+        back(o03_1, 0, 1, 0)
+        nc.scalar.copy(out=osb[0][:, 0:512], in_=o03_0[:])
+        mul(d03_1, 3, 1, 3)
+        back(o03_1, 1, 1, 1)
+        back(o03_1, 2, 1, 2)
+        mul(e45_1, 2, 1, 4)
+        back(o03_1, 3, 1, 3)
+        mul(e45_1, 3, 1, 5)
         o45_1 = bank(3, "o45_1")
-        for j in range(2):
-            back(o45_1, j, 1, 4 + j)
+        back(o45_1, 0, 1, 4)
+        nc.vector.tensor_tensor(out=osb[1][:, 0:512], in0=o03_1[:], in1=w0b[:, 0:512], op=ALU.add)
+        nc.sync.dma_start(out=out[0:P, :], in_=osb[0][:])
+        back(o45_1, 1, 1, 5)
         nc.vector.tensor_tensor(out=osb[1][:, 512:768], in0=o45_1[:, 0:256], in1=w0b[:, 512:768], op=ALU.add)
+        nc.sync.dma_start(out=out[P : 2 * P, 0:512], in_=osb[1][:, 0:512])
         nc.sync.dma_start(out=out[P : 2 * P, 512:768], in_=osb[1][:, 512:768])

@@ -48,28 +48,27 @@ def tile_metalinearheadml_pb_w4_kernel(
         w = sb([P, G2, 4 * E], U8, "w")
         vrow = sb([P, HD], BF16, "vrow")
         identb = sb([P, P], BF16, "identb")
-        w0b = sb([P, E], BF16, "w0b")
         zero = sb([P, 512], BF16, "zero")
+        brow = sb([P, P], BF16, "brow")
         bcol = sb([P, 3, NE], F32, "bcol")
         one = sb([P, 1], F32, "one")
         ident = sb([P, P], F32, "ident")
 
-        nc.vector.memset(warm[:], 0.0)
-        nc.scalar.activation(out=warm[:, 1:2], in_=warm[:, 0:1], func=ACT.Sigmoid)
-        nc.vector.memset(zero[:], 0.0)
-        nc.vector.memset(one[:], 1.0)
-        nc.vector.memset(vrow[:], 0.0)
+        nc.vector.memset(vrow[:].bitcast(I32), 0)
         nc.vector.memset(psi_sc[:].rearrange("p g n -> p (g n)").bitcast(I32), 0)
+        nc.vector.memset(zero[:].bitcast(I32), 0)
+        nc.vector.memset(one[:], 1.0)
+        nc.vector.memset(warm[:], 0.0)
         nc.vector.memset(w_sc[:].rearrange("p g n -> p (g n)").bitcast(I32), 0)
+        nc.vector.memset(brow[:].bitcast(I32), 0)
         make_identity(nc, ident[:])
-        nc.gpsimd.dma_start(out=vrow[0:1, :], in_=psi_b1.unsqueeze(0))
-        for i, vec in enumerate((b_gate, b_dw, W0)):
-            nc.gpsimd.dma_start(out=vrow[1 + NE * i : 1 + NE * (i + 1), 0:P], in_=vec.rearrange("(j p) -> j p", p=P))
 
         nc.sync.dma_start(out=rb8[0][:, 0:512], in_=r_bytes[0:P, 0:512])
+        nc.scalar.dma_start(out=rsc[:], in_=r_scale.rearrange("o (g p t) -> p (o g) t", p=P, t=4))
+        nc.scalar.activation(out=warm[:, 1:2], in_=warm[:, 0:1], func=ACT.Sigmoid)
         nc.sync.dma_start(out=rb8[0][:, 512:2048], in_=r_bytes[0:P, 512:2048])
-        nc.sync.dma_start(out=rsc[:], in_=r_scale.rearrange("o (g p t) -> p (o g) t", p=P, t=4))
         nc.sync.dma_start(out=rb8[1][:], in_=r_bytes[P : 2 * P, :])
+        nc.sync.dma_start(out=vrow[0:1, :], in_=psi_b1.unsqueeze(0))
         for q in range(4):
             nc.sync.dma_start(
                 out=psi_sc[32 * q : 32 * q + 4, :, :].bitcast(I32),
@@ -77,6 +76,8 @@ def tile_metalinearheadml_pb_w4_kernel(
             )
         for g in range(G1):
             nc.sync.dma_start(out=psi[:, g, :].bitcast(I32), in_=psi_w1_words[g].bitcast(I32))
+        for i, vec in enumerate((b_gate, b_dw, W0)):
+            nc.sync.dma_start(out=brow[NE * i : NE * (i + 1), :], in_=vec.rearrange("(j p) -> j p", p=P))
         for k, words, sc in ((0, w_gate_words, w_gate_scales), (1, w_dw_words, w_dw_scales)):
             nc.sync.dma_start(
                 out=w[:, :, 2 * E * k : 2 * E * (k + 1)].bitcast(I32), in_=words.rearrange("g p n -> p g n").bitcast(I32)
@@ -86,7 +87,6 @@ def tile_metalinearheadml_pb_w4_kernel(
                     out=w_sc[32 * q : 32 * q + 4, :, E * k : E * (k + 1)].bitcast(I32),
                     in_=sc[:, 4 * q : 4 * q + 4, :].rearrange("g q n -> q g n").bitcast(I32),
                 )
-        nc.sync.dma_start(out=w0b[:], in_=W0.partition_broadcast(P))
         nc.vector.tensor_copy(out=identb[:], in_=ident[:])
 
         def spread(row, lo, hi, ps):
@@ -233,6 +233,11 @@ def tile_metalinearheadml_pb_w4_kernel(
                 op1=ALU.mult,
             )
 
+        def addw0v(c, j):
+            nc.vector.tensor_scalar(
+                out=z[c, j][:], in0=z[c, j][:], scalar1=bcol[:, 2, j : j + 1], scalar2=None, op0=ALU.add
+            )
+
         def addw0(c, j):
             nc.gpsimd.tensor_scalar(
                 out=z[c, j][:], in0=z[c, j][:], scalar1=1.0, scalar2=bcol[:, 2, j : j + 1], op0=ALU.mult, op1=ALU.add
@@ -245,152 +250,158 @@ def tile_metalinearheadml_pb_w4_kernel(
         nc.tensor.matmul(out=wm[:], lhsT=zero[:, 0:P], rhs=zero[:], start=True, stop=True)
         nc.tensor.matmul(out=wm[:], lhsT=zero[:, 0:P], rhs=zero[:], start=True, stop=True)
         nc.tensor.matmul(out=wm[:], lhsT=zero[:, 0:P], rhs=zero[:], start=True, stop=True)
+        nc.tensor.matmul(out=wm[:], lhsT=zero[:, 0:P], rhs=zero[:], start=True, stop=True)
         cast(0, 0, "v")
         cast(0, 1, "v")
-        cast(0, 3, "s")
+        cast(0, 2, "s")
         turn(0, 0)
         scale(0, 0)
         turn(0, 1)
         cast(1, 1, "s")
-        nc.tensor.matmul(out=wm[:], lhsT=zero[:, 0:P], rhs=zero[:], start=True, stop=True)
+        turn(0, 2)
+        scale(0, 1)
         sp1 = bank(7, "sp1")
         spread(0, 512, 1024, sp1)
-        scale(0, 1)
-        cast(0, 2, "s")
-        turn(0, 3)
-        quant(0, 0)
-        turn(1, 1)
-        cast(1, 0, "s")
-        quant(0, 1)
-        turn(0, 2)
-        scale(0, 3)
-        nc.scalar.copy(out=b1[:, 512:1024], in_=sp1[:])
-        stage1(0, 0)
-        scale(0, 2)
+        cast(0, 3, "s")
         sp0 = bank(6, "sp0")
         spread(0, 0, 512, sp0)
+        scale(0, 2)
+        turn(1, 1)
+        cast(1, 0, "s")
+        turn(0, 3)
+        quant(0, 1)
         cast(1, 2, "s")
-        scale(1, 1)
-        bt = psum.tile([P, 1024], BF16, name="bt", tag="bank7")
-        nc.tensor.transpose(bt[:, 0:P], vrow[:, 0:P], identb[:])
+        quant(0, 0)
         turn(1, 0)
+        scale(0, 3)
+        stage1(0, 0)
         cast(1, 3, "s")
-        turn(1, 2)
         quant(0, 2)
         stage1(0, 1)
-        scale(1, 0)
-        nc.scalar.copy(out=b1[:, 0:512], in_=sp0[:])
-        stage1(0, 2)
         quant(0, 3)
-        nc.scalar.copy(out=bcol[:], in_=bt[:, 1 : 1 + 3 * NE].rearrange("p (v j) -> p v j", v=3))
-        quant(1, 0)
-        quant(1, 1)
+        nc.scalar.copy(out=b1[:, 512:1024], in_=sp1[:])
+        scale(1, 1)
+        stage1(0, 2)
+        nc.scalar.copy(out=b1[:, 0:512], in_=sp0[:])
+        scale(1, 0)
         stage1(0, 3)
+        quant(1, 1)
+        bias(0, 0)
+        turn(1, 2)
+        turn(1, 3)
+        quant(1, 0)
+        bt = psum.tile([P, 1024], BF16, name="bt", tag="bank7")
+        nc.tensor.transpose(bt[:, 0:P], brow[:], identb[:])
+        hturn(0, 0, 0)
         scale(1, 2)
         stage1(1, 0)
-        bias(0, 1)
-        turn(1, 3)
-        bias(0, 0)
-        hturn(0, 1, 1)
-        stage1(1, 1)
-        relu(0, 1)
-        quant(1, 2)
-        scale(1, 3)
-        hturn(0, 0, 0)
-        stage1(1, 2)
         relu(0, 0)
+        bias(0, 1)
+        stage1(1, 1)
+        quant(1, 2)
+        hturn(0, 1, 1)
+        scale(1, 3)
+        nc.scalar.copy(out=bcol[:], in_=bt[:, 0 : 3 * NE].rearrange("p (v j) -> p v j", v=3))
+        stage1(1, 2)
+        relu(0, 1)
         quant(1, 3)
-        hquant(0, 1)
-        stage1(1, 3)
         hquant(0, 0)
+        stage1(1, 3)
+        hquant(0, 1)
         bias(1, 0)
-        g03_0 = bank(4, "g03_0")
-        product(g03_0, 0, 0, 0, 0)
-        product(g03_0, 1, 0, 0, 1)
-        product(g03_0, 2, 0, 0, 2)
         e45_0 = bank(0, "e45_0")
         product(e45_0, 0, 0, 0, 4)
-        bias(1, 1)
-        hturn(1, 0, 2)
         d03_0 = bank(5, "d03_0")
         product(d03_0, 0, 0, 1, 0)
+        g03_0 = bank(4, "g03_0")
+        product(g03_0, 0, 0, 0, 0)
+        product(e45_0, 1, 0, 0, 5)
+        bias(1, 1)
+        hturn(1, 0, 2)
+        product(g03_0, 1, 0, 0, 1)
         relu(1, 0)
         hturn(1, 1, 3)
-        product(g03_0, 3, 0, 0, 3)
+        product(g03_0, 2, 0, 0, 2)
         relu(1, 1)
-        product(e45_0, 1, 0, 0, 5)
-        hquant(1, 0)
         product(d03_0, 1, 0, 1, 1)
-        product(e45_0, 2, 0, 1, 4)
+        hquant(1, 0)
         product(d03_0, 2, 0, 1, 2)
-        sig(g03_0, 1, 0, 1)
+        product(g03_0, 3, 0, 0, 3)
+        product(e45_0, 2, 0, 1, 4)
         hquant(1, 1)
-        product(d03_0, 3, 0, 1, 3)
-        sig(g03_0, 2, 0, 2)
         product(e45_0, 3, 0, 1, 5)
         sig(g03_0, 0, 0, 0)
+        product(d03_0, 3, 0, 1, 3)
+        sig(g03_0, 1, 0, 1)
+        d03_1 = bank(7, "d03_1")
+        product(d03_1, 0, 1, 1, 0)
+        sig(g03_0, 2, 0, 2)
         g03_1 = bank(6, "g03_1")
         product(g03_1, 0, 1, 0, 0)
         mul(d03_0, 1, 0, 1)
         sig(g03_0, 3, 0, 3)
         product(g03_1, 1, 1, 0, 1)
-        mul(d03_0, 0, 0, 0)
-        sig(e45_0, 0, 0, 4)
-        product(g03_1, 2, 1, 0, 2)
         mul(d03_0, 2, 0, 2)
+        sig(e45_0, 0, 0, 4)
+        addw0(0, 1)
+        product(g03_1, 2, 1, 0, 2)
+        mul(d03_0, 3, 0, 3)
         sig(e45_0, 1, 0, 5)
         product(g03_1, 3, 1, 0, 3)
-        addw0(0, 0)
-        mul(d03_0, 3, 0, 3)
-        e45_1 = bank(2, "e45_1")
-        product(e45_1, 0, 1, 0, 4)
         addw0(0, 2)
-        mul(e45_0, 3, 0, 5)
-        d03_1 = bank(7, "d03_1")
-        product(d03_1, 0, 1, 1, 0)
-        sig(g03_1, 2, 1, 2)
-        product(e45_1, 1, 1, 0, 5)
+        mul(d03_0, 0, 0, 0)
+        product(d03_1, 1, 1, 1, 1)
         mul(e45_0, 2, 0, 4)
         addw0(0, 3)
-        sig(g03_1, 3, 1, 3)
-        product(d03_1, 1, 1, 1, 1)
-        sig(g03_1, 0, 1, 0)
-        addw0(0, 4)
-        product(e45_1, 2, 1, 1, 4)
-        product(e45_1, 3, 1, 1, 5)
-        addw0(0, 5)
         product(d03_1, 2, 1, 1, 2)
-        addw0(0, 1)
+        sig(g03_1, 1, 1, 1)
         product(d03_1, 3, 1, 1, 3)
-        sig(e45_1, 1, 1, 5)
-        sig(e45_1, 0, 1, 4)
+        mul(e45_0, 3, 0, 5)
+        sig(g03_1, 0, 1, 0)
+        addw0(0, 0)
+        e45_1 = bank(2, "e45_1")
+        product(e45_1, 0, 1, 0, 4)
+        sig(g03_1, 3, 1, 3)
+        addw0(0, 4)
+        product(e45_1, 1, 1, 0, 5)
+        mul(d03_1, 0, 1, 0)
+        sig(g03_1, 2, 1, 2)
+        product(e45_1, 2, 1, 1, 4)
+        mul(d03_1, 1, 1, 1)
+        addw0(0, 5)
+        product(e45_1, 3, 1, 1, 5)
+        mul(d03_1, 3, 1, 3)
         o45_0 = bank(4, "o45_0")
         back(o45_0, 0, 0, 4)
+        addw0v(1, 0)
         back(o45_0, 1, 0, 5)
-        mul(d03_1, 2, 1, 2)
-        sig(g03_1, 1, 1, 1)
+        sig(e45_1, 0, 1, 4)
+        addw0v(1, 1)
         o03_0 = bank(1, "o03_0")
         back(o03_0, 0, 0, 0)
         back(o03_0, 1, 0, 1)
-        mul(d03_1, 0, 1, 0)
+        sig(e45_1, 1, 1, 5)
+        mul(d03_1, 2, 1, 2)
         back(o03_0, 2, 0, 2)
-        nc.scalar.copy(out=osb[0][:, 512:768], in_=o45_0[:, 0:256])
         back(o03_0, 3, 0, 3)
-        mul(d03_1, 1, 1, 1)
+        nc.scalar.copy(out=osb[0][:, 512:768], in_=o45_0[:, 0:256])
         o03_1 = bank(0, "o03_1")
         back(o03_1, 0, 1, 0)
-        nc.scalar.copy(out=osb[0][:, 0:512], in_=o03_0[:])
-        mul(d03_1, 3, 1, 3)
         back(o03_1, 1, 1, 1)
-        back(o03_1, 2, 1, 2)
-        mul(e45_1, 2, 1, 4)
-        back(o03_1, 3, 1, 3)
         mul(e45_1, 3, 1, 5)
+        addw0v(1, 3)
+        nc.scalar.copy(out=osb[0][:, 0:512], in_=o03_0[:])
+        addw0v(1, 2)
+        mul(e45_1, 2, 1, 4)
+        back(o03_1, 2, 1, 2)
+        back(o03_1, 3, 1, 3)
+        addw0v(1, 5)
+        addw0v(1, 4)
+        nc.sync.dma_start(out=out[0:P, :], in_=osb[0][:])
+        nc.scalar.copy(out=osb[1][:, 0:512], in_=o03_1[:])
         o45_1 = bank(3, "o45_1")
         back(o45_1, 0, 1, 4)
-        nc.vector.tensor_tensor(out=osb[1][:, 0:512], in0=o03_1[:], in1=w0b[:, 0:512], op=ALU.add)
-        nc.sync.dma_start(out=out[0:P, :], in_=osb[0][:])
         back(o45_1, 1, 1, 5)
-        nc.vector.tensor_tensor(out=osb[1][:, 512:768], in0=o45_1[:, 0:256], in1=w0b[:, 512:768], op=ALU.add)
+        nc.vector.tensor_copy(out=osb[1][:, 512:768], in_=o45_1[:, 0:256])
         nc.sync.dma_start(out=out[P : 2 * P, 0:512], in_=osb[1][:, 0:512])
         nc.sync.dma_start(out=out[P : 2 * P, 512:768], in_=osb[1][:, 512:768])

@@ -196,6 +196,16 @@ def tile_metalinearheadml_pb_w4_kernel(
                 func=ACT.Relu,
             )
 
+        def reluv(c, g):
+            hgrp[c, g] = sb([P, 512], BF16, "hgrp_%d_%d" % (c, g))
+            nc.vector.tensor_scalar(
+                out=hgrp[c, g][:].rearrange("p (c u e) -> p c u e", u=2, e=2),
+                in0=ht[c, g][:, 0:256].bitcast(BF16).rearrange("p (u c e) -> p c u e", u=2, e=2),
+                scalar1=0.0,
+                scalar2=None,
+                op0=ALU.max,
+            )
+
         def hquant(c, g):
             nc.vector.quantize_mx(out=hq[:, c, g, :].bitcast(FP8X4), scales=hqs[:, c, g, :], in_=hgrp[c, g][:])
 
@@ -246,119 +256,121 @@ def tile_metalinearheadml_pb_w4_kernel(
         def back(ps, slot, c, j):
             nc.tensor.transpose(ps[:, P * slot : P * (slot + 1)], z[c, j][:], ident[:])
 
+        def wmm(i):
+            nc.tensor.matmul(out=wm[:], lhsT=zero[:, 0:P], rhs=zero[:], start=True, stop=True)
+
         wm = bank(7, "wm")
-        nc.tensor.matmul(out=wm[:], lhsT=zero[:, 0:P], rhs=zero[:], start=True, stop=True)
-        nc.tensor.matmul(out=wm[:], lhsT=zero[:, 0:P], rhs=zero[:], start=True, stop=True)
-        nc.tensor.matmul(out=wm[:], lhsT=zero[:, 0:P], rhs=zero[:], start=True, stop=True)
-        nc.tensor.matmul(out=wm[:], lhsT=zero[:, 0:P], rhs=zero[:], start=True, stop=True)
+        wmm(0)
+        wmm(1)
+        wmm(2)
         cast(0, 0, "v")
         cast(0, 1, "v")
         cast(0, 2, "s")
         turn(0, 0)
         scale(0, 0)
         turn(0, 1)
-        cast(1, 1, "s")
+        cast(0, 3, "s")
         turn(0, 2)
         scale(0, 1)
-        sp1 = bank(7, "sp1")
-        spread(0, 512, 1024, sp1)
-        cast(0, 3, "s")
         sp0 = bank(6, "sp0")
         spread(0, 0, 512, sp0)
-        scale(0, 2)
-        turn(1, 1)
         cast(1, 0, "s")
         turn(0, 3)
-        quant(0, 1)
-        cast(1, 2, "s")
         quant(0, 0)
+        cast(1, 1, "s")
+        scale(0, 2)
         turn(1, 0)
-        scale(0, 3)
-        stage1(0, 0)
-        cast(1, 3, "s")
-        quant(0, 2)
-        stage1(0, 1)
-        quant(0, 3)
-        nc.scalar.copy(out=b1[:, 512:1024], in_=sp1[:])
-        scale(1, 1)
-        stage1(0, 2)
+        sp1 = bank(7, "sp1")
+        spread(0, 512, 1024, sp1)
         nc.scalar.copy(out=b1[:, 0:512], in_=sp0[:])
         scale(1, 0)
-        stage1(0, 3)
-        quant(1, 1)
-        bias(0, 0)
-        turn(1, 2)
-        turn(1, 3)
+        stage1(0, 0)
+        cast(1, 3, "s")
+        quant(0, 1)
+        turn(1, 1)
+        quant(0, 2)
         quant(1, 0)
-        bt = psum.tile([P, 1024], BF16, name="bt", tag="bank7")
+        cast(1, 2, "s")
+        stage1(0, 1)
+        scale(0, 3)
+        nc.scalar.copy(out=b1[:, 512:1024], in_=sp1[:])
+        turn(1, 2)
+        scale(1, 1)
+        stage1(0, 2)
+        quant(0, 3)
+        scale(1, 2)
+        stage1(0, 3)
+        bias(0, 0)
+        stage1(1, 0)
+        bias(0, 1)
+        bt = psum.tile([P, 1024], BF16, name="bt", tag="bank2")
         nc.tensor.transpose(bt[:, 0:P], brow[:], identb[:])
         hturn(0, 0, 0)
-        scale(1, 2)
-        stage1(1, 0)
+        turn(1, 3)
         relu(0, 0)
-        bias(0, 1)
-        stage1(1, 1)
-        quant(1, 2)
+        quant(1, 1)
         hturn(0, 1, 1)
+        quant(1, 2)
+        stage1(1, 1)
         scale(1, 3)
-        nc.scalar.copy(out=bcol[:], in_=bt[:, 0 : 3 * NE].rearrange("p (v j) -> p v j", v=3))
-        stage1(1, 2)
         relu(0, 1)
+        stage1(1, 2)
+        nc.scalar.copy(out=bcol[:], in_=bt[:, 0 : 3 * NE].rearrange("p (v j) -> p v j", v=3))
         quant(1, 3)
         hquant(0, 0)
         stage1(1, 3)
         hquant(0, 1)
         bias(1, 0)
-        e45_0 = bank(0, "e45_0")
-        product(e45_0, 0, 0, 0, 4)
-        d03_0 = bank(5, "d03_0")
-        product(d03_0, 0, 0, 1, 0)
         g03_0 = bank(4, "g03_0")
         product(g03_0, 0, 0, 0, 0)
-        product(e45_0, 1, 0, 0, 5)
-        bias(1, 1)
-        hturn(1, 0, 2)
-        product(g03_0, 1, 0, 0, 1)
-        relu(1, 0)
-        hturn(1, 1, 3)
-        product(g03_0, 2, 0, 0, 2)
-        relu(1, 1)
+        d03_0 = bank(5, "d03_0")
+        product(d03_0, 0, 0, 1, 0)
         product(d03_0, 1, 0, 1, 1)
-        hquant(1, 0)
-        product(d03_0, 2, 0, 1, 2)
+        e45_0 = bank(0, "e45_0")
+        product(e45_0, 0, 0, 0, 4)
+        bias(1, 1)
+        product(g03_0, 1, 0, 0, 1)
+        hturn(1, 0, 2)
+        hturn(1, 1, 3)
+        relu(1, 0)
+        product(g03_0, 2, 0, 0, 2)
+        reluv(1, 1)
+        product(e45_0, 1, 0, 0, 5)
         product(g03_0, 3, 0, 0, 3)
         product(e45_0, 2, 0, 1, 4)
-        hquant(1, 1)
-        product(e45_0, 3, 0, 1, 5)
-        sig(g03_0, 0, 0, 0)
-        product(d03_0, 3, 0, 1, 3)
+        hquant(1, 0)
+        product(d03_0, 2, 0, 1, 2)
         sig(g03_0, 1, 0, 1)
-        d03_1 = bank(7, "d03_1")
-        product(d03_1, 0, 1, 1, 0)
+        product(d03_0, 3, 0, 1, 3)
+        hquant(1, 1)
+        sig(g03_0, 0, 0, 0)
+        product(e45_0, 3, 0, 1, 5)
         sig(g03_0, 2, 0, 2)
         g03_1 = bank(6, "g03_1")
         product(g03_1, 0, 1, 0, 0)
-        mul(d03_0, 1, 0, 1)
-        sig(g03_0, 3, 0, 3)
-        product(g03_1, 1, 1, 0, 1)
-        mul(d03_0, 2, 0, 2)
-        sig(e45_0, 0, 0, 4)
-        addw0(0, 1)
-        product(g03_1, 2, 1, 0, 2)
-        mul(d03_0, 3, 0, 3)
-        sig(e45_0, 1, 0, 5)
-        product(g03_1, 3, 1, 0, 3)
-        addw0(0, 2)
         mul(d03_0, 0, 0, 0)
+        product(g03_1, 1, 1, 0, 1)
+        sig(e45_0, 0, 0, 4)
+        mul(d03_0, 1, 0, 1)
+        addw0(0, 0)
+        product(g03_1, 2, 1, 0, 2)
+        sig(g03_0, 3, 0, 3)
+        d03_1 = bank(7, "d03_1")
+        product(d03_1, 0, 1, 1, 0)
+        sig(e45_0, 1, 0, 5)
+        addw0(0, 1)
+        product(g03_1, 3, 1, 0, 3)
+        mul(d03_0, 3, 0, 3)
         product(d03_1, 1, 1, 1, 1)
-        mul(e45_0, 2, 0, 4)
+        mul(d03_0, 2, 0, 2)
         addw0(0, 3)
         product(d03_1, 2, 1, 1, 2)
-        sig(g03_1, 1, 1, 1)
-        product(d03_1, 3, 1, 1, 3)
-        mul(e45_0, 3, 0, 5)
         sig(g03_1, 0, 1, 0)
-        addw0(0, 0)
+        mul(e45_0, 2, 0, 4)
+        product(d03_1, 3, 1, 1, 3)
+        sig(g03_1, 1, 1, 1)
+        addw0(0, 2)
+        mul(e45_0, 3, 0, 5)
         e45_1 = bank(2, "e45_1")
         product(e45_1, 0, 1, 0, 4)
         sig(g03_1, 3, 1, 3)
@@ -367,40 +379,41 @@ def tile_metalinearheadml_pb_w4_kernel(
         mul(d03_1, 0, 1, 0)
         sig(g03_1, 2, 1, 2)
         product(e45_1, 2, 1, 1, 4)
-        mul(d03_1, 1, 1, 1)
         addw0(0, 5)
+        mul(d03_1, 1, 1, 1)
         product(e45_1, 3, 1, 1, 5)
-        mul(d03_1, 3, 1, 3)
-        o45_0 = bank(4, "o45_0")
-        back(o45_0, 0, 0, 4)
         addw0v(1, 0)
-        back(o45_0, 1, 0, 5)
-        sig(e45_1, 0, 1, 4)
-        addw0v(1, 1)
+        mul(d03_1, 2, 1, 2)
         o03_0 = bank(1, "o03_0")
         back(o03_0, 0, 0, 0)
         back(o03_0, 1, 0, 1)
-        sig(e45_1, 1, 1, 5)
-        mul(d03_1, 2, 1, 2)
+        sig(e45_1, 0, 1, 4)
+        mul(d03_1, 3, 1, 3)
         back(o03_0, 2, 0, 2)
         back(o03_0, 3, 0, 3)
-        nc.scalar.copy(out=osb[0][:, 512:768], in_=o45_0[:, 0:256])
+        sig(e45_1, 1, 1, 5)
         o03_1 = bank(0, "o03_1")
         back(o03_1, 0, 1, 0)
-        back(o03_1, 1, 1, 1)
-        mul(e45_1, 3, 1, 5)
-        addw0v(1, 3)
-        nc.scalar.copy(out=osb[0][:, 0:512], in_=o03_0[:])
+        addw0v(1, 1)
+        o45_0 = bank(4, "o45_0")
+        back(o45_0, 0, 0, 4)
         addw0v(1, 2)
-        mul(e45_1, 2, 1, 4)
+        nc.scalar.copy(out=osb[0][:, 0:512], in_=o03_0[:])
+        back(o03_1, 1, 1, 1)
+        addw0v(1, 3)
+        back(o45_0, 1, 0, 5)
         back(o03_1, 2, 1, 2)
+        mul(e45_1, 2, 1, 4)
         back(o03_1, 3, 1, 3)
-        addw0v(1, 5)
+        mul(e45_1, 3, 1, 5)
+        nc.scalar.copy(out=osb[0][:, 512:768], in_=o45_0[:, 0:256])
         addw0v(1, 4)
-        nc.sync.dma_start(out=out[0:P, :], in_=osb[0][:])
+        nc.sync.dma_start(out=out[0:P, 0:512], in_=osb[0][:, 0:512])
+        addw0v(1, 5)
         nc.scalar.copy(out=osb[1][:, 0:512], in_=o03_1[:])
         o45_1 = bank(3, "o45_1")
         back(o45_1, 0, 1, 4)
+        nc.sync.dma_start(out=out[0:P, 512:768], in_=osb[0][:, 512:768])
         back(o45_1, 1, 1, 5)
         nc.vector.tensor_copy(out=osb[1][:, 512:768], in_=o45_1[:, 0:256])
         nc.sync.dma_start(out=out[P : 2 * P, 0:512], in_=osb[1][:, 0:512])

from contextlib import ExitStack

import concourse.mybir as mybir
from concourse.masks import make_identity

S_CLS, R, HD, E = 256, 2048, 1024, 768
FLOPS = 2 * S_CLS * R * HD + 2 * S_CLS * HD * 2 * E

F32 = mybir.dt.float32
BF16 = mybir.dt.bfloat16
U32 = mybir.dt.uint32
I32 = mybir.dt.int32
U8 = mybir.dt.uint8
F8 = mybir.dt.float8_e4m3fn
FP8X4 = mybir.dt.float8_e4m3fn_x4
FP4X4 = mybir.dt.float4_e2m1fn_x4
ACT = mybir.ActivationFunctionType
ALU = mybir.AluOpType

P = 128
G1 = R // 512
G2 = HD // 512
NE = E // P


def tile_metalinearheadml_pb_w4_kernel(
    tc, r_bytes, r_scale, psi_w1_words, psi_w1_scales, psi_b1, w_dw_words, w_dw_scales, b_dw, w_gate_words, w_gate_scales, b_gate, W0, out
):
    nc = tc.nc
    with ExitStack() as ctx:
        keep = ctx.enter_context(tc.tile_pool(name="keep", bufs=1))
        psum = ctx.enter_context(tc.psum_pool(name="psum", bufs=1))
        ctx.enter_context(tc.manual_schedule())

        def sb(shape, dt, name):
            return keep.tile(shape, dt, name=name, tag=name, align_bytes=256)

        def bank(i, name):
            return psum.tile([P, 512], F32, name=name, tag="bank%d" % i)

        warm = sb([P, 8], F32, "warm")
        psi_sc = sb([P, G1, HD], U8, "psi_sc")
        w_sc = sb([P, G2, 2 * E], U8, "w_sc")
        rb8 = [sb([P, R], U8, "rb8_%d" % c) for c in range(2)]
        rsc = sb([P, G1, 4], F32, "rsc")
        psi = sb([P, G1, 2 * HD], U8, "psi")
        b1 = sb([P, HD], BF16, "b1")
        w = sb([P, G2, 4 * E], U8, "w")
        vrow = sb([P, HD], BF16, "vrow")
        identb = sb([P, P], BF16, "identb")
        zero = sb([P, 512], BF16, "zero")
        brow = sb([P, P], BF16, "brow")
        bcol = sb([P, 3, NE], F32, "bcol")
        one = sb([P, 1], F32, "one")
        ident = sb([P, P], F32, "ident")

        nc.vector.memset(vrow[:].bitcast(I32), 0)
        nc.vector.memset(psi_sc[:].rearrange("p g n -> p (g n)").bitcast(I32), 0)
        nc.vector.memset(zero[:].bitcast(I32), 0)
        nc.vector.memset(one[:], 1.0)
        nc.vector.memset(warm[:], 0.0)
        nc.vector.memset(w_sc[:].rearrange("p g n -> p (g n)").bitcast(I32), 0)
        nc.vector.memset(brow[:].bitcast(I32), 0)
        make_identity(nc, ident[:])

        nc.sync.dma_start(out=rb8[0][:, 0:512], in_=r_bytes[0:P, 0:512])
        nc.scalar.dma_start(out=rsc[:], in_=r_scale.rearrange("o (g p t) -> p (o g) t", p=P, t=4))
        nc.scalar.activation(out=warm[:, 1:2], in_=warm[:, 0:1], func=ACT.Sigmoid)
        nc.sync.dma_start(out=rb8[0][:, 512:2048], in_=r_bytes[0:P, 512:2048])
        nc.sync.dma_start(out=rb8[1][:], in_=r_bytes[P : 2 * P, :])
        nc.sync.dma_start(out=vrow[0:1, :], in_=psi_b1.unsqueeze(0))
        for q in range(4):
            nc.sync.dma_start(
                out=psi_sc[32 * q : 32 * q + 4, :, :].bitcast(I32),
                in_=psi_w1_scales[:, 4 * q : 4 * q + 4, :].rearrange("g q n -> q g n").bitcast(I32),
            )
        for g in range(G1):
            nc.sync.dma_start(out=psi[:, g, :].bitcast(I32), in_=psi_w1_words[g].bitcast(I32))
        for i, vec in enumerate((b_gate, b_dw, W0)):
            nc.sync.dma_start(out=brow[NE * i : NE * (i + 1), :], in_=vec.rearrange("(j p) -> j p", p=P))
        for k, words, sc in ((0, w_gate_words, w_gate_scales), (1, w_dw_words, w_dw_scales)):
            nc.sync.dma_start(
                out=w[:, :, 2 * E * k : 2 * E * (k + 1)].bitcast(I32), in_=words.rearrange("g p n -> p g n").bitcast(I32)
            )
            for q in range(4):
                nc.sync.dma_start(
                    out=w_sc[32 * q : 32 * q + 4, :, E * k : E * (k + 1)].bitcast(I32),
                    in_=sc[:, 4 * q : 4 * q + 4, :].rearrange("g q n -> q g n").bitcast(I32),
                )
        nc.vector.tensor_copy(out=identb[:], in_=ident[:])

        def spread(row, lo, hi, ps):
            nc.tensor.matmul(
                out=ps[:, 0 : hi - lo],
                lhsT=identb[:, row : row + 1].to_broadcast([P, P]),
                rhs=vrow[:, lo:hi],
                start=True,
                stop=True,
            )

        rbf = [sb([P, R], BF16, "rbf_%d" % c) for c in range(2)]
        rq = sb([P, 2, G1, P], U32, "rq")
        rqs = sb([P, 2, G1, P], U8, "rqs")
        grp = {}
        xt = {}
        acc = {}

        split = set()

        def cast(c, g, eng):
            src = rb8[c][:, 512 * g : 512 * (g + 1)].bitcast(F8)
            dst = rbf[c][:, 512 * g : 512 * (g + 1)]
            if eng == "v":
                nc.vector.tensor_scalar(
                    out=dst.rearrange("p (u w e) -> p w u e", u=2, e=2),
                    in0=src.rearrange("p (w u e) -> p w u e", u=2, e=2),
                    scalar1=one[:],
                    scalar2=None,
                    op0=ALU.mult,
                )
                split.add((c, g))
            else:
                nc.scalar.copy(out=dst, in_=src)

        def turn(c, g):
            words = rbf[c][:].bitcast(F32)
            xt[c, g] = bank(g, "xt_%d_%d" % (c, g))
            for u in range(2):
                if (c, g) in split:
                    cols = words[:, 256 * g + P * u : 256 * g + P * (u + 1)]
                else:
                    cols = words[:, 256 * g + u : 256 * (g + 1) : 2]
                nc.tensor.transpose(xt[c, g][:, P * u : P * (u + 1)], cols, ident[:])

        def scale(c, g):
            if (c, g // 2) not in grp:
                grp[c, g // 2] = sb([P, 2, 512], BF16, "grp_%d_%d" % (c, g // 2))
            nc.vector.tensor_tensor(
                out=grp[c, g // 2][:, g % 2, :].rearrange("p (c u e) -> p c u e", u=2, e=2),
                in0=xt[c, g][:, 0:256].bitcast(BF16).rearrange("p (u c e) -> p c u e", u=2, e=2),
                in1=rsc[:, g, :].rearrange("p (u e) -> p u e", e=2).unsqueeze(1).to_broadcast([P, P, 2, 2]),
                op=ALU.mult,
            )

        def quant(c, g):
            nc.vector.quantize_mx(out=rq[:, c, g, :].bitcast(FP8X4), scales=rqs[:, c, g, :], in_=grp[c, g // 2][:, g % 2, :])

        def quant2(c, h):
            gs = slice(2 * h, 2 * h + 2)
            nc.vector.quantize_mx(
                out=rq[:, c, gs, :].rearrange("p g n -> p (g n)").bitcast(FP8X4),
                scales=rqs[:, c, gs, :].rearrange("p g n -> p (g n)"),
                in_=grp[c, h][:].rearrange("p g n -> p (g n)"),
            )

        def stage1(c, g):
            for h in range(2):
                if g == 0:
                    acc[c, h] = bank(4 + 2 * c + h, "acc_%d_%d" % (c, h))
                nc.tensor.matmul_mx(
                    out=acc[c, h][:],
                    lhsT=rq[:, c, g, :].bitcast(FP8X4),
                    lhsT_scale=rqs[:, c, g, :],
                    rhs=psi[:, g, 1024 * h : 1024 * (h + 1)].bitcast(FP4X4),
                    rhs_scale=psi_sc[:, g, 512 * h : 512 * (h + 1)],
                    start=(g == 0),
                    stop=(g == G1 - 1),
                )

        hbf = [sb([P, HD], BF16, "hbf_%d" % c) for c in range(2)]
        hq = sb([P, 2, G2, P], U32, "hq")
        hqs = sb([P, 2, G2, P], U8, "hqs")
        ht = {}
        hgrp = {}

        def bias(c, h):
            cols = slice(512 * h, 512 * (h + 1))
            nc.vector.tensor_tensor(
                out=hbf[c][:, cols].rearrange("p (u w e) -> p w u e", u=2, e=2),
                in0=acc[c, h][:].rearrange("p (w u e) -> p w u e", u=2, e=2),
                in1=b1[:, cols].rearrange("p (w u e) -> p w u e", u=2, e=2),
                op=ALU.add,
            )

        def hturn(c, g, b):
            words = hbf[c][:].bitcast(F32)
            ht[c, g] = bank(b, "ht_%d_%d" % (c, g))
            for u in range(2):
                nc.tensor.transpose(ht[c, g][:, P * u : P * (u + 1)], words[:, 256 * g + P * u : 256 * g + P * (u + 1)], ident[:])

        def relu(c, g):
            hgrp[c, g] = sb([P, 512], BF16, "hgrp_%d_%d" % (c, g))
            nc.scalar.activation(
                out=hgrp[c, g][:].rearrange("p (c u e) -> p c u e", u=2, e=2),
                in_=ht[c, g][:, 0:256].bitcast(BF16).rearrange("p (u c e) -> p c u e", u=2, e=2),
                func=ACT.Relu,
            )

        def reluv(c, g):
            hgrp[c, g] = sb([P, 512], BF16, "hgrp_%d_%d" % (c, g))
            nc.vector.tensor_scalar(
                out=hgrp[c, g][:].rearrange("p (c u e) -> p c u e", u=2, e=2),
                in0=ht[c, g][:, 0:256].bitcast(BF16).rearrange("p (u c e) -> p c u e", u=2, e=2),
                scalar1=0.0,
                scalar2=None,
                op0=ALU.max,
            )

        def hquant(c, g):
            nc.vector.quantize_mx(out=hq[:, c, g, :].bitcast(FP8X4), scales=hqs[:, c, g, :], in_=hgrp[c, g][:])

        def product(ps, slot, c, kind, j):
            for g in range(G2):
                col = E * kind + P * j
                nc.tensor.matmul_mx(
                    out=ps[:, P * slot : P * (slot + 1)],
                    lhsT=w[:, g, 2 * col : 2 * (col + P)].bitcast(FP4X4),
                    lhsT_scale=w_sc[:, g, col : col + P],
                    rhs=hq[:, c, g, :].bitcast(FP8X4),
                    rhs_scale=hqs[:, c, g, :],
                    start=(g == 0),
                    stop=(g == G2 - 1),
                )

        gate = {}
        z = {}
        osb = [sb([P, E], F32, "osb_%d" % c) for c in range(2)]

        def sig(ps, slot, c, j):
            gate[c, j] = sb([P, P], F32, "gate_%d_%d" % (c, j))
            nc.scalar.activation(
                out=gate[c, j][:], in_=ps[:, P * slot : P * (slot + 1)], func=ACT.Sigmoid, bias=bcol[:, 0, j : j + 1]
            )

        def mul(ps, slot, c, j):
            z[c, j] = sb([P, P], F32, "z_%d_%d" % (c, j))
            nc.vector.scalar_tensor_tensor(
                out=z[c, j][:],
                in0=ps[:, P * slot : P * (slot + 1)],
                scalar=bcol[:, 1, j : j + 1],
                in1=gate[c, j][:],
                op0=ALU.add,
                op1=ALU.mult,
            )

        def addw0v(c, j):
            nc.vector.tensor_scalar(
                out=z[c, j][:], in0=z[c, j][:], scalar1=bcol[:, 2, j : j + 1], scalar2=None, op0=ALU.add
            )

        def addw0(c, j):
            nc.gpsimd.tensor_scalar(
                out=z[c, j][:], in0=z[c, j][:], scalar1=1.0, scalar2=bcol[:, 2, j : j + 1], op0=ALU.mult, op1=ALU.add
            )

        def back(ps, slot, c, j):
            nc.tensor.transpose(ps[:, P * slot : P * (slot + 1)], z[c, j][:], ident[:])

        def wmm(i):
            nc.tensor.matmul(out=wm[:], lhsT=zero[:, 0:P], rhs=zero[:], start=True, stop=True)

        wm = bank(7, "wm")
        wmm(0)
        wmm(1)
        wmm(2)
        cast(0, 0, "v")
        cast(0, 1, "v")
        cast(0, 2, "s")
        turn(0, 0)
        scale(0, 0)
        turn(0, 1)
        cast(0, 3, "s")
        turn(0, 2)
        scale(0, 1)
        sp0 = bank(6, "sp0")
        spread(0, 0, 512, sp0)
        cast(1, 0, "s")
        turn(0, 3)
        quant(0, 0)
        cast(1, 1, "s")
        scale(0, 2)
        turn(1, 0)
        sp1 = bank(7, "sp1")
        spread(0, 512, 1024, sp1)
        nc.scalar.copy(out=b1[:, 0:512], in_=sp0[:])
        scale(1, 0)
        stage1(0, 0)
        cast(1, 3, "s")
        quant(0, 1)
        turn(1, 1)
        quant(0, 2)
        quant(1, 0)
        cast(1, 2, "s")
        stage1(0, 1)
        scale(0, 3)
        nc.scalar.copy(out=b1[:, 512:1024], in_=sp1[:])
        turn(1, 2)
        scale(1, 1)
        stage1(0, 2)
        quant(0, 3)
        scale(1, 2)
        stage1(0, 3)
        bias(0, 0)
        stage1(1, 0)
        bias(0, 1)
        bt = psum.tile([P, 1024], BF16, name="bt", tag="bank2")
        nc.tensor.transpose(bt[:, 0:P], brow[:], identb[:])
        hturn(0, 0, 0)
        turn(1, 3)
        relu(0, 0)
        quant(1, 1)
        hturn(0, 1, 1)
        quant(1, 2)
        stage1(1, 1)
        scale(1, 3)
        relu(0, 1)
        stage1(1, 2)
        nc.scalar.copy(out=bcol[:], in_=bt[:, 0 : 3 * NE].rearrange("p (v j) -> p v j", v=3))
        quant(1, 3)
        hquant(0, 0)
        stage1(1, 3)
        hquant(0, 1)
        bias(1, 0)
        g03_0 = bank(4, "g03_0")
        product(g03_0, 0, 0, 0, 0)
        d03_0 = bank(5, "d03_0")
        product(d03_0, 0, 0, 1, 0)
        product(d03_0, 1, 0, 1, 1)
        e45_0 = bank(0, "e45_0")
        product(e45_0, 0, 0, 0, 4)
        bias(1, 1)
        product(g03_0, 1, 0, 0, 1)
        hturn(1, 0, 2)
        hturn(1, 1, 3)
        relu(1, 0)
        product(g03_0, 2, 0, 0, 2)
        reluv(1, 1)
        product(e45_0, 1, 0, 0, 5)
        product(g03_0, 3, 0, 0, 3)
        product(e45_0, 2, 0, 1, 4)
        hquant(1, 0)
        product(d03_0, 2, 0, 1, 2)
        sig(g03_0, 1, 0, 1)
        product(d03_0, 3, 0, 1, 3)
        hquant(1, 1)
        sig(g03_0, 0, 0, 0)
        product(e45_0, 3, 0, 1, 5)
        sig(g03_0, 2, 0, 2)
        g03_1 = bank(6, "g03_1")
        product(g03_1, 0, 1, 0, 0)
        mul(d03_0, 0, 0, 0)
        product(g03_1, 1, 1, 0, 1)
        sig(e45_0, 0, 0, 4)
        mul(d03_0, 1, 0, 1)
        addw0(0, 0)
        product(g03_1, 2, 1, 0, 2)
        sig(g03_0, 3, 0, 3)
        d03_1 = bank(7, "d03_1")
        product(d03_1, 0, 1, 1, 0)
        sig(e45_0, 1, 0, 5)
        addw0(0, 1)
        product(g03_1, 3, 1, 0, 3)
        mul(d03_0, 3, 0, 3)
        product(d03_1, 1, 1, 1, 1)
        mul(d03_0, 2, 0, 2)
        addw0(0, 3)
        product(d03_1, 2, 1, 1, 2)
        sig(g03_1, 0, 1, 0)
        mul(e45_0, 2, 0, 4)
        product(d03_1, 3, 1, 1, 3)
        sig(g03_1, 1, 1, 1)
        addw0(0, 2)
        mul(e45_0, 3, 0, 5)
        e45_1 = bank(2, "e45_1")
        product(e45_1, 0, 1, 0, 4)
        sig(g03_1, 3, 1, 3)
        addw0(0, 4)
        product(e45_1, 1, 1, 0, 5)
        mul(d03_1, 0, 1, 0)
        sig(g03_1, 2, 1, 2)
        product(e45_1, 2, 1, 1, 4)
        addw0(0, 5)
        mul(d03_1, 1, 1, 1)
        product(e45_1, 3, 1, 1, 5)
        addw0v(1, 0)
        mul(d03_1, 2, 1, 2)
        o03_0 = bank(1, "o03_0")
        back(o03_0, 0, 0, 0)
        back(o03_0, 1, 0, 1)
        sig(e45_1, 0, 1, 4)
        mul(d03_1, 3, 1, 3)
        back(o03_0, 2, 0, 2)
        back(o03_0, 3, 0, 3)
        sig(e45_1, 1, 1, 5)
        o03_1 = bank(0, "o03_1")
        back(o03_1, 0, 1, 0)
        addw0v(1, 1)
        o45_0 = bank(4, "o45_0")
        back(o45_0, 0, 0, 4)
        addw0v(1, 2)
        nc.scalar.copy(out=osb[0][:, 0:512], in_=o03_0[:])
        back(o03_1, 1, 1, 1)
        addw0v(1, 3)
        back(o45_0, 1, 0, 5)
        back(o03_1, 2, 1, 2)
        mul(e45_1, 2, 1, 4)
        back(o03_1, 3, 1, 3)
        mul(e45_1, 3, 1, 5)
        nc.scalar.copy(out=osb[0][:, 512:768], in_=o45_0[:, 0:256])
        addw0v(1, 4)
        nc.sync.dma_start(out=out[0:P, 0:512], in_=osb[0][:, 0:512])
        addw0v(1, 5)
        nc.scalar.copy(out=osb[1][:, 0:512], in_=o03_1[:])
        o45_1 = bank(3, "o45_1")
        back(o45_1, 0, 1, 4)
        nc.sync.dma_start(out=out[0:P, 512:768], in_=osb[0][:, 512:768])
        back(o45_1, 1, 1, 5)
        nc.vector.tensor_copy(out=osb[1][:, 512:768], in_=o45_1[:, 0:256])
        nc.sync.dma_start(out=out[P : 2 * P, 0:512], in_=osb[1][:, 0:512])
        nc.sync.dma_start(out=out[P : 2 * P, 512:768], in_=osb[1][:, 512:768])
